import numpy as np
import ml_dtypes


def mxq(x, axis, fmt="e4m3"):
    dtype, down = {"e4m3": (ml_dtypes.float8_e4m3fn, 7), "e5m2": (ml_dtypes.float8_e5m2, 14)}[fmt]
    v = np.moveaxis(np.asarray(x, np.float32).astype(ml_dtypes.bfloat16).astype(np.float64), axis, -1)
    blocks = v.reshape(v.shape[:-1] + (-1, 32))
    amax = np.abs(blocks).max(-1, keepdims=True)
    byte = np.maximum(np.where(amax > 0, np.frexp(amax)[1] - 1 + 127, 0) - down, 1)
    scale = np.exp2(byte - 127.0)
    codes = (blocks / scale).astype(np.float32).astype(dtype).astype(np.float64)
    return np.moveaxis((codes * scale).reshape(v.shape), -1, axis)


WIDE = False


def mx_kscale(k):
    if not WIDE:
        return np.ones(k)
    levels = np.array([10, -10, 5, -5, 0])
    a = np.random.permutation(np.resize(levels, k // 512 * 4)).reshape(k // 512, 4)
    idx = np.arange(k)
    return np.exp2(a[idx // 512, idx % 128 // 32])


BF16 = ml_dtypes.bfloat16


def bf(x):
    return np.asarray(x, np.float32).astype(BF16)


def f64(x):
    return np.asarray(x).astype(np.float64)


B, R, C, O, I = 1024, 8, 16, 16, 1024
EPS = 1e-8
ROUTING_ITERS = 3


def squash(s):
    norm = np.sqrt((s * s).sum(axis=-1, keepdims=True))
    return norm / (1.0 + norm * norm + EPS) * s


def softmax(b, axis):
    e = np.exp(b - b.max(axis=axis, keepdims=True))
    return e / e.sum(axis=axis, keepdims=True)


def setup_inputs():
    s = mx_kscale(I)
    return {"x": bf(np.random.standard_normal((B, R, I)) * s),
            "W": bf(np.random.standard_normal((R, C, O, I)) * (C / np.sqrt(R * O * I)) / s),
            "bias": bf(np.random.standard_normal((1, 1, C, O)) * 0.4 / np.sqrt(O))}


def reference(x, W, bias):
    xq = mxq(f64(x), 2, "e4m3")
    Wq = mxq(f64(W), 3, "e4m3")
    bias = f64(bias)
    u = xq.transpose(1, 0, 2) @ Wq.reshape(R, C * O, I).transpose(0, 2, 1)
    u_hat = u.transpose(1, 0, 2).reshape(B, R, C, O)
    b_ij = np.zeros((B, R, C, 1))
    v_j = None
    for itr in range(ROUTING_ITERS):
        c_ij = softmax(b_ij, 2)
        s_j = (c_ij * u_hat).sum(axis=1, keepdims=True) + bias
        v_j = squash(s_j)
        if itr < ROUTING_ITERS - 1:
            a_ij = (u_hat * v_j).sum(axis=-1, keepdims=True)
            b_ij = b_ij + a_ij
    return v_j[:, 0]

@@ -1,0 +1,354 @@
+from contextlib import ExitStack
+
+import concourse.mybir as mybir
+from concourse.masks import make_identity
+
+F32 = mybir.dt.float32
+BF16 = mybir.dt.bfloat16
+U32 = mybir.dt.uint32
+U8 = mybir.dt.uint8
+FP8X4 = mybir.dt.float8_e4m3fn_x4
+ALU = mybir.AluOpType
+ACT = mybir.ActivationFunctionType
+AX = mybir.AxisListType
+
+FLOPS = 2 * 1024 * 8 * 256 * 1024
+
+P = 128
+NU = 4
+EPS = 1e-8
+
+PE_RED = True
+S_MULT_ENG = "GGGG"
+A_MULT_ENG = "VVVV"
+X_EVAC = "SSSV"
+W_EVAC = "SV"
+
+
+def tile_capsulelayer_t_kernel(tc, x, W, bias, out):
+    nc = tc.nc
+    with ExitStack() as ctx:
+        const = ctx.enter_context(tc.tile_pool(name="const", bufs=1))
+        xin_pool = ctx.enter_context(tc.tile_pool(name="xin", bufs=4))
+        grp_pool = ctx.enter_context(tc.tile_pool(name="grp", bufs=2))
+        xq_pool = ctx.enter_context(tc.tile_pool(name="xq", bufs=2))
+        u_pool = ctx.enter_context(tc.tile_pool(name="u", bufs=4))
+        p_pool = ctx.enter_context(tc.tile_pool(name="p", bufs=2))
+        sm = ctx.enter_context(tc.tile_pool(name="sm", bufs=2))
+        keep = ctx.enter_context(tc.tile_pool(name="keep", bufs=4))
+        ps_tp = ctx.enter_context(tc.psum_pool(name="pstp", bufs=2))
+        ps_u = ctx.enter_context(tc.psum_pool(name="psu", bufs=2))
+        ps_acc = ctx.enter_context(tc.psum_pool(name="psacc", bufs=2))
+        ps_back = ctx.enter_context(tc.psum_pool(name="psback", bufs=2))
+
+        def copy_on(letter, dst, src):
+            if letter == "S":
+                nc.scalar.copy(out=dst, in_=src)
+            else:
+                nc.vector.tensor_copy(out=dst, in_=src)
+
+        ident = const.tile([P, P], F32, name="ident")
+        make_identity(nc, ident[:])
+        tinyb = const.tile([P, 1], F32, name="tinyb")
+        nc.vector.memset(tinyb[:], 1e-30)
+        braw = const.tile([P, 256], BF16, name="braw")
+        nc.sync.dma_start(out=braw[:], in_=bias.rearrange("a b c o -> (a b c o)").partition_broadcast(P))
+        bc = const.tile([P, 256], F32, name="bc")
+        nc.vector.tensor_copy(
+            out=bc[:].rearrange("p (o c) -> p o c", c=16),
+            in_=braw[:].rearrange("p (c o) -> p o c", o=16),
+        )
+        wc = const.tile([P, 8, 512], U32, name="wc", align_bytes=64)
+        ws = const.tile([P, 8, 512], U8, name="ws", align_bytes=64)
+        bias_t = const.tile([P, 2], F32, name="bias_t")
+        if PE_RED:
+            tpb = ps_tp.tile([P, 4, P], F32, tag="tp", name="tpb")
+            for h in range(2):
+                nc.tensor.transpose(out=tpb[:, h, :], in_=bc[:, h * P:(h + 1) * P], identity=ident[:])
+            for h in range(2):
+                nc.vector.tensor_copy(out=bias_t[:, h:h + 1], in_=tpb[:, h, 0:1])
+
+        w_rows = W.rearrange("r c o i -> (r c o) i")
+
+        def load_w(wq):
+            win = xin_pool.tile([P, 4096], BF16, tag="xin", name="win")
+            nc.sync.dma_start(
+                out=win[:].rearrange("p (t i) -> p t i", t=4),
+                in_=w_rows[wq * 512:(wq + 1) * 512, :].rearrange("(t p) i -> p t i", p=P),
+            )
+            return win
+
+        def prep_w(wq, win):
+            ww = win[:].bitcast(F32)
+            grp = grp_pool.tile([P, 4096], BF16, tag="grp", name="grpw", align_bytes=64)
+            gv = grp[:].bitcast(F32).rearrange("p (r g o c u) -> p r g o c u", r=2, g=2, o=16, c=16, u=2)
+            for rl in range(2):
+                for h in range(2):
+                    t = rl * 2 + h
+                    tp = ps_tp.tile([P, 4, P], F32, tag="tp", name="tpw")
+                    for k in range(4):
+                        nc.tensor.transpose(
+                            out=tp[:, k, :], in_=ww[:, t * 512 + k * P: t * 512 + (k + 1) * P], identity=ident[:]
+                        )
+                    for g in range(2):
+                        copy_on(
+                            W_EVAC[g],
+                            gv[:, rl, g, :, 8 * h:8 * h + 8, :],
+                            tp[:, 2 * g:2 * g + 2, :].rearrange("p u (c o) -> p o c u", o=16),
+                        )
+            nc.vector.quantize_mx(
+                out=wc[:, 2 * wq:2 * wq + 2, :].rearrange("p a b -> p (a b)").bitcast(FP8X4),
+                scales=ws[:, 2 * wq:2 * wq + 2, :].rearrange("p a b -> p (a b)"),
+                in_=grp[:],
+            )
+
+        def load_x(t, half):
+            xin = xin_pool.tile([P, 4096], BF16, tag="xin", name="xin")
+            nc.sync.dma_start(
+                out=xin[:],
+                in_=x[t * P:(t + 1) * P, 4 * half:4 * half + 4, :].rearrange("b r i -> b (r i)"),
+            )
+            return xin
+
+        def prep_x(xin, xc, xs, half):
+            xw = xin[:].bitcast(F32)
+            grp = grp_pool.tile([P, 4096], BF16, tag="grp", name="grpx", align_bytes=64)
+            gv = grp[:].bitcast(F32).rearrange("p (r g b u) -> p r g b u", r=4, g=2, b=P, u=2)
+            for rl in range(4):
+                tp = ps_tp.tile([P, 4, P], F32, tag="tp", name="tpx")
+                for k in range(4):
+                    nc.tensor.transpose(
+                        out=tp[:, k, :], in_=xw[:, rl * 512 + k * P: rl * 512 + (k + 1) * P], identity=ident[:]
+                    )
+                copy_on(X_EVAC[rl], gv[:, rl], tp[:].rearrange("p (g u) b -> p g b u", u=2))
+            nc.vector.quantize_mx(
+                out=xc[:, 8 * half:8 * half + 8, :].rearrange("p a b -> p (a b)").bitcast(FP8X4),
+                scales=xs[:, 8 * half:8 * half + 8, :].rearrange("p a b -> p (a b)"),
+                in_=grp[:],
+            )
+
+        def mx_half(xc, xs, u, j, half):
+            for jr in range(2 * half, 2 * half + 2):
+                ups = ps_u.tile([P, 512], F32, tag="ups", name="ups")
+                for rr in range(2):
+                    r = 2 * jr + rr
+                    for g in range(2):
+                        nc.tensor.matmul_mx(
+                            out=ups[:, rr * 256:(rr + 1) * 256],
+                            lhsT=xc[:, 2 * r + g, :].bitcast(FP8X4),
+                            lhsT_scale=xs[:, 2 * r + g, :],
+                            rhs=wc[:, r, g * 256:(g + 1) * 256].bitcast(FP8X4),
+                            rhs_scale=ws[:, r, g * 256:(g + 1) * 256],
+                            start=(g == 0),
+                            stop=(g == 1),
+                        )
+                nc.scalar.copy(out=u[:, j * 2048 + jr * 512: j * 2048 + (jr + 1) * 512], in_=ups[:])
+
+        st = [dict() for q in range(NU)]
+
+        def front_unit(q):
+            u = u_pool.tile([P, 4096], F32, tag="u", name="u")
+            st[q]["u"] = u
+            for j in range(2):
+                t = 2 * q + j
+                xc = xq_pool.tile([P, 16, P], U32, tag="xc", name="xc", align_bytes=64)
+                xs = xq_pool.tile([P, 16, P], U8, tag="xs", name="xs", align_bytes=64)
+                if t == 0:
+                    w0 = load_w(0)
+                    x0 = load_x(0, 0)
+                    w1 = load_w(1)
+                    prep_w(0, w0)
+                    prep_x(x0, xc, xs, 0)
+                    w2 = load_w(2)
+                    prep_w(1, w1)
+                    mx_half(xc, xs, u, j, 0)
+                    x1 = load_x(0, 1)
+                    w3 = load_w(3)
+                    prep_w(2, w2)
+                    prep_x(x1, xc, xs, 1)
+                    prep_w(3, w3)
+                    mx_half(xc, xs, u, j, 1)
+                else:
+                    for half in range(2):
+                        xin = load_x(t, half)
+                        prep_x(xin, xc, xs, half)
+                        mx_half(xc, xs, u, j, half)
+
+        def acc_transposes(dst, srcs):
+            n = len(srcs)
+            for i in range(n):
+                nc.tensor.matmul(
+                    out=dst, lhsT=srcs[i], rhs=ident[:], is_transpose=True, start=(i == 0), stop=(i == n - 1)
+                )
+
+        def reduce_routes(src, scale):
+            if PE_RED:
+                sv = src[:].rearrange("p (j r h k) -> p j r h k", j=2, r=8, h=2)
+                acc = ps_acc.tile([P, 2, 2, P], F32, tag="acc", name="acc_s")
+                for j in range(2):
+                    for h in range(2):
+                        acc_transposes(acc[:, j, h, :], [sv[:, j, r, h, :] for r in range(8)])
+                s_t = sm.tile([P, 2, 2, P], F32, tag="s_t", name="s_t")
+                for h in range(2):
+                    nc.scalar.activation(
+                        out=s_t[:, :, h, :], in_=acc[:, :, h, :], func=ACT.Identity,
+                        bias=bias_t[:, h:h + 1], scale=scale,
+                    )
+                back = ps_back.tile([P, 512], F32, tag="back", name="back_s")
+                for j in range(2):
+                    for h in range(2):
+                        nc.tensor.transpose(
+                            out=back[:, (2 * j + h) * P:(2 * j + h + 1) * P], in_=s_t[:, j, h, :], identity=ident[:]
+                        )
+                return back
+            red = sm.tile([P, 512], F32, tag="red", name="red")
+            s_sb = sm.tile([P, 512], F32, tag="s_sb", name="s_sb")
+            for j in range(2):
+                nc.vector.tensor_reduce(
+                    out=red[:, j * 256:(j + 1) * 256],
+                    in_=src[:, j * 2048:(j + 1) * 2048].rearrange("p (r k) -> p k r", r=8),
+                    axis=AX.X, op=ALU.add,
+                )
+                nc.vector.scalar_tensor_tensor(
+                    out=s_sb[:, j * 256:(j + 1) * 256], in0=red[:, j * 256:(j + 1) * 256], scalar=scale,
+                    in1=bc[:], op0=ALU.mult, op1=ALU.add,
+                )
+            return s_sb
+
+        def squash_gain(s):
+            sq = sm.tile([P, 512], F32, tag="sq", name="sq")
+            nc.scalar.activation(out=sq[:], in_=s[:], func=ACT.Square)
+            n2 = sm.tile([P, 32], F32, tag="n2", name="n2")
+            nc.vector.tensor_reduce(
+                out=n2[:].rearrange("p (j c) -> p j c", j=2),
+                in_=sq[:].rearrange("p (j o c) -> p j c o", j=2, c=16),
+                axis=AX.X, op=ALU.add,
+            )
+            nn = sm.tile([P, 32], F32, tag="nn", name="nn")
+            nc.scalar.activation(out=nn[:], in_=n2[:], func=ACT.Sqrt, bias=tinyb[:, 0:1])
+            dd = sm.tile([P, 32], F32, tag="dd", name="dd")
+            nc.vector.tensor_scalar(out=dd[:], in0=n2[:], scalar1=1.0 + EPS, scalar2=None, op0=ALU.add)
+            rd = sm.tile([P, 32], F32, tag="rd", name="rd")
+            nc.vector.reciprocal(out=rd[:], in_=dd[:])
+            gain = keep.tile([P, 32], F32, tag="gain", name="gain")
+            nc.vector.tensor_mul(out=gain[:], in0=nn[:], in1=rd[:])
+            return gain
+
+        def stage_s(q, k):
+            u = st[q]["u"]
+            if k == 0:
+                s = reduce_routes(u, 1.0 / 16.0)
+            else:
+                cc = st[q]["c"]
+                ps = p_pool.tile([P, 4096], F32, tag="p", name="p_s")
+                pv = ps[:].rearrange("p (a h o c) -> p a h o c", a=16, h=2, c=16)
+                uv = u[:].rearrange("p (a h o c) -> p a h o c", a=16, h=2, c=16)
+                cv = cc[:].rearrange("p (a c) -> p a c", c=16)
+                for j in range(2):
+                    for h in range(2):
+                        eng = nc.gpsimd if S_MULT_ENG[2 * j + h] == "G" else nc.vector
+                        eng.tensor_tensor(
+                            out=pv[:, 8 * j:8 * j + 8, h],
+                            in0=uv[:, 8 * j:8 * j + 8, h],
+                            in1=cv[:, 8 * j:8 * j + 8, :].unsqueeze(2).to_broadcast([P, 8, 8, 16]),
+                            op=ALU.mult,
+                        )
+                s = reduce_routes(ps, 1.0)
+            st[q]["s"] = s
+            gain = squash_gain(s)
+            st[q]["gain"] = gain
+            if k == 2:
+                vo = sm.tile([P, 512], F32, tag="vo", name="vo")
+                nc.vector.tensor_tensor(
+                    out=vo[:].rearrange("p (j c o) -> p j c o", j=2, o=16),
+                    in0=s[:].rearrange("p (j o c) -> p j c o", j=2, c=16),
+                    in1=gain[:].rearrange("p (j c) -> p j c", j=2).unsqueeze(3).to_broadcast([P, 2, 16, 16]),
+                    op=ALU.mult,
+                )
+                nc.sync.dma_start(
+                    out=out[q * 256:(q + 1) * 256].rearrange("(j b) c o -> b j (c o)", j=2),
+                    in_=vo[:].rearrange("p (j k) -> p j k", j=2),
+                )
+
+        def stage_a(q, k):
+            u = st[q]["u"]
+            s = st[q]["s"]
+            gain = st[q]["gain"]
+            pa = p_pool.tile([P, 4096], F32, tag="p", name="p_a")
+            pv = pa[:].rearrange("p (j o r c) -> p j o r c", j=2, o=16, c=16)
+            uv = u[:].rearrange("p (j r o c) -> p j o r c", j=2, r=8, c=16)
+            sv = s[:].rearrange("p (j o c) -> p j o c", j=2, c=16)
+            for j in range(2):
+                for oh in range(2):
+                    nc.vector.tensor_tensor(
+                        out=pv[:, j, 8 * oh:8 * oh + 8],
+                        in0=uv[:, j, 8 * oh:8 * oh + 8],
+                        in1=sv[:, j, 8 * oh:8 * oh + 8, :].unsqueeze(2).to_broadcast([P, 8, 8, 16]),
+                        op=ALU.mult,
+                    )
+            if PE_RED:
+                pk = pa[:].rearrange("p (j o k) -> p j o k", j=2, o=16)
+                acc = ps_acc.tile([P, 2, P], F32, tag="acc", name="acc_a")
+                for j in range(2):
+                    acc_transposes(acc[:, j, :], [pk[:, j, o, :] for o in range(16)])
+                a_t = sm.tile([P, 2, P], F32, tag="a_t", name="a_t")
+                nc.scalar.copy(out=a_t[:], in_=acc[:])
+                araw = ps_back.tile([P, 256], F32, tag="back", name="back_a")
+                for j in range(2):
+                    nc.tensor.transpose(out=araw[:, j * P:(j + 1) * P], in_=a_t[:, j, :], identity=ident[:])
+            else:
+                araw = sm.tile([P, 256], F32, tag="a_sb", name="a_sb")
+                for j in range(2):
+                    nc.vector.tensor_reduce(
+                        out=araw[:, j * P:(j + 1) * P],
+                        in_=pa[:, j * 2048:(j + 1) * 2048].rearrange("p (o k) -> p k o", o=16),
+                        axis=AX.X, op=ALU.add,
+                    )
+            gv = gain[:].rearrange("p (j c) -> p j c", j=2).unsqueeze(2).to_broadcast([P, 2, 8, 16])
+            logit = keep.tile([P, 256], F32, tag="logit%d" % k, name="logit")
+            if k == 0:
+                nc.vector.tensor_tensor(
+                    out=logit[:].rearrange("p (j r c) -> p j r c", j=2, c=16),
+                    in0=araw[:].rearrange("p (j r c) -> p j r c", j=2, c=16), in1=gv, op=ALU.mult,
+                )
+            else:
+                tmp = sm.tile([P, 256], F32, tag="tmp", name="tmp")
+                nc.vector.tensor_tensor(
+                    out=tmp[:].rearrange("p (j r c) -> p j r c", j=2, c=16),
+                    in0=araw[:].rearrange("p (j r c) -> p j r c", j=2, c=16), in1=gv, op=ALU.mult,
+                )
+                nc.vector.tensor_add(out=logit[:], in0=tmp[:], in1=st[q]["logit"][:])
+            st[q]["logit"] = logit
+            lv = logit[:].rearrange("p (a c) -> p a c", c=16)
+            nmax = sm.tile([P, 16], F32, tag="nmax", name="nmax")
+            nc.vector.tensor_reduce(out=nmax[:], in_=lv, axis=AX.X, op=ALU.max)
+            sh = sm.tile([P, 256], F32, tag="sh", name="sh")
+            nc.vector.tensor_tensor(
+                out=sh[:].rearrange("p (a c) -> p a c", c=16), in0=lv,
+                in1=nmax[:].unsqueeze(2).to_broadcast([P, 16, 16]), op=ALU.subtract,
+            )
+            ex = sm.tile([P, 256], F32, tag="ex", name="ex")
+            nc.scalar.activation(out=ex[:], in_=sh[:], func=ACT.Exp)
+            ev = ex[:].rearrange("p (a c) -> p a c", c=16)
+            esum = sm.tile([P, 16], F32, tag="esum", name="esum")
+            nc.vector.tensor_reduce(out=esum[:], in_=ev, axis=AX.X, op=ALU.add)
+            rs = sm.tile([P, 16], F32, tag="rs", name="rs")
+            nc.vector.reciprocal(out=rs[:], in_=esum[:])
+            cc = keep.tile([P, 256], F32, tag="cc", name="cc")
+            nc.vector.tensor_tensor(
+                out=cc[:].rearrange("p (a c) -> p a c", c=16), in0=ev,
+                in1=rs[:].unsqueeze(2).to_broadcast([P, 16, 16]), op=ALU.mult,
+            )
+            st[q]["c"] = cc
+
+        for slot in range(NU + 3):
+            if slot < NU:
+                front_unit(slot)
+            if 0 <= slot - 1 < NU:
+                stage_s(slot - 1, 0)
+                stage_a(slot - 1, 0)
+            if 0 <= slot - 2 < NU:
+                stage_s(slot - 2, 1)
+                stage_a(slot - 2, 1)
+            if 0 <= slot - 3 < NU:
+                stage_s(slot - 3, 2)

@@ -178,7 +178,7 @@ def tile_capsulelayer_t_kernel(tc, x, W, bias, out):
             n = len(srcs)
             for i in range(n):
                 nc.tensor.matmul(
-                    out=dst, lhsT=srcs[i], rhs=ident[:], is_transpose=True, start=(i == 0), stop=(i == n - 1)
+                    out=dst, lhsT=srcs[i], rhs=ident[:], is_transpose=(i % 8 != 3), start=(i == 0), stop=(i == n - 1)
                 )
 
         def reduce_routes(src, scale):

@@ -18,28 +18,27 @@ P = 128
 NU = 4
 EPS = 1e-8
 
-PE_RED = True
-S_MULT_ENG = "GGGG"
-A_MULT_ENG = "VVVV"
+MANUAL = False
+RATE = 3
 X_EVAC = "SSSV"
 W_EVAC = "SV"
+S_MULT = "GGGG"
+REG_EVERY = 0
+SH_BUFS = 5
+LG_BUFS = 3
+BIG_BUFS = 6
 
 
 def tile_capsulelayer_t_kernel(tc, x, W, bias, out):
     nc = tc.nc
     with ExitStack() as ctx:
         const = ctx.enter_context(tc.tile_pool(name="const", bufs=1))
-        xin_pool = ctx.enter_context(tc.tile_pool(name="xin", bufs=4))
-        grp_pool = ctx.enter_context(tc.tile_pool(name="grp", bufs=2))
+        big = ctx.enter_context(tc.tile_pool(name="big", bufs=BIG_BUFS))
         xq_pool = ctx.enter_context(tc.tile_pool(name="xq", bufs=2))
         u_pool = ctx.enter_context(tc.tile_pool(name="u", bufs=4))
-        p_pool = ctx.enter_context(tc.tile_pool(name="p", bufs=2))
-        sm = ctx.enter_context(tc.tile_pool(name="sm", bufs=2))
-        keep = ctx.enter_context(tc.tile_pool(name="keep", bufs=4))
-        ps_tp = ctx.enter_context(tc.psum_pool(name="pstp", bufs=2))
-        ps_u = ctx.enter_context(tc.psum_pool(name="psu", bufs=2))
-        ps_acc = ctx.enter_context(tc.psum_pool(name="psacc", bufs=2))
-        ps_back = ctx.enter_context(tc.psum_pool(name="psback", bufs=2))
+        un = ctx.enter_context(tc.tile_pool(name="un", bufs=4))
+        ps_sh = ctx.enter_context(tc.psum_pool(name="pssh", bufs=SH_BUFS))
+        ps_lg = ctx.enter_context(tc.psum_pool(name="pslg", bufs=LG_BUFS))
 
         def copy_on(letter, dst, src):
             if letter == "S":
@@ -61,31 +60,38 @@ def tile_capsulelayer_t_kernel(tc, x, W, bias, out):
         wc = const.tile([P, 8, 512], U32, name="wc", align_bytes=64)
         ws = const.tile([P, 8, 512], U8, name="ws", align_bytes=64)
         bias_t = const.tile([P, 2], F32, name="bias_t")
-        if PE_RED:
-            tpb = ps_tp.tile([P, 4, P], F32, tag="tp", name="tpb")
-            for h in range(2):
-                nc.tensor.transpose(out=tpb[:, h, :], in_=bc[:, h * P:(h + 1) * P], identity=ident[:])
-            for h in range(2):
-                nc.vector.tensor_copy(out=bias_t[:, h:h + 1], in_=tpb[:, h, 0:1])
+        tpb = ps_sh.tile([P, 4, P], F32, tag="sh", name="tpb")
+        for h in range(2):
+            nc.tensor.transpose(out=tpb[:, h, :], in_=bc[:, h * P:(h + 1) * P], identity=ident[:])
+        for h in range(2):
+            nc.vector.tensor_copy(out=bias_t[:, h:h + 1], in_=tpb[:, h, 0:1])
+
+        if MANUAL:
+            ctx.enter_context(tc.manual_schedule())
 
         w_rows = W.rearrange("r c o i -> (r c o) i")
+        fe = dict()
+        st = [dict() for q in range(NU)]
 
-        def load_w(wq):
-            win = xin_pool.tile([P, 4096], BF16, tag="xin", name="win")
+        def load_w(wt):
+            win = big.tile([P, 8192], BF16, tag="big", name="win", align_bytes=64)
             nc.sync.dma_start(
-                out=win[:].rearrange("p (t i) -> p t i", t=4),
-                in_=w_rows[wq * 512:(wq + 1) * 512, :].rearrange("(t p) i -> p t i", p=P),
+                out=win[:].rearrange("p (t i) -> p t i", t=8),
+                in_=w_rows[wt * 1024:(wt + 1) * 1024, :].rearrange("(t p) i -> p t i", p=P),
             )
-            return win
+            fe["w%d" % wt] = win
 
-        def prep_w(wq, win):
-            ww = win[:].bitcast(F32)
-            grp = grp_pool.tile([P, 4096], BF16, tag="grp", name="grpw", align_bytes=64)
-            gv = grp[:].bitcast(F32).rearrange("p (r g o c u) -> p r g o c u", r=2, g=2, o=16, c=16, u=2)
-            for rl in range(2):
+        def w_step(wq):
+            wt, sub = divmod(wq, 2)
+            if sub == 0:
+                fe["gw%d" % wt] = big.tile([P, 8192], BF16, tag="big", name="grpw", align_bytes=64)
+            ww = fe["w%d" % wt][:].bitcast(F32)
+            grp = fe["gw%d" % wt]
+            gv = grp[:].bitcast(F32).rearrange("p (r g o c u) -> p r g o c u", r=4, g=2, o=16, c=16, u=2)
+            for rl in range(2 * sub, 2 * sub + 2):
                 for h in range(2):
                     t = rl * 2 + h
-                    tp = ps_tp.tile([P, 4, P], F32, tag="tp", name="tpw")
+                    tp = ps_sh.tile([P, 4, P], F32, tag="sh", name="tpw")
                     for k in range(4):
                         nc.tensor.transpose(
                             out=tp[:, k, :], in_=ww[:, t * 512 + k * P: t * 512 + (k + 1) * P], identity=ident[:]
@@ -99,256 +105,293 @@ def tile_capsulelayer_t_kernel(tc, x, W, bias, out):
             nc.vector.quantize_mx(
                 out=wc[:, 2 * wq:2 * wq + 2, :].rearrange("p a b -> p (a b)").bitcast(FP8X4),
                 scales=ws[:, 2 * wq:2 * wq + 2, :].rearrange("p a b -> p (a b)"),
-                in_=grp[:],
+                in_=grp[:, sub * 4096:(sub + 1) * 4096],
             )
 
-        def load_x(t, half):
-            xin = xin_pool.tile([P, 4096], BF16, tag="xin", name="xin")
-            nc.sync.dma_start(
-                out=xin[:],
-                in_=x[t * P:(t + 1) * P, 4 * half:4 * half + 4, :].rearrange("b r i -> b (r i)"),
-            )
-            return xin
+        def load_x(t):
+            xin = big.tile([P, 8192], BF16, tag="big", name="xin", align_bytes=64)
+            for half in range(2):
+                nc.sync.dma_start(
+                    out=xin[:, half * 4096:(half + 1) * 4096],
+                    in_=x[t * P:(t + 1) * P, 4 * half:4 * half + 4, :].rearrange("b r i -> b (r i)"),
+                )
+            fe["x%d" % t] = xin
 
-        def prep_x(xin, xc, xs, half):
-            xw = xin[:].bitcast(F32)
-            grp = grp_pool.tile([P, 4096], BF16, tag="grp", name="grpx", align_bytes=64)
-            gv = grp[:].bitcast(F32).rearrange("p (r g b u) -> p r g b u", r=4, g=2, b=P, u=2)
-            for rl in range(4):
-                tp = ps_tp.tile([P, 4, P], F32, tag="tp", name="tpx")
+        def fe_transposes(i, pair):
+            t, half = divmod(i, 2)
+            xw = fe["x%d" % t][:].bitcast(F32)
+            gv = fe["g%d" % t][:].bitcast(F32).rearrange("p (r g b u) -> p r g b u", r=8, g=2, b=P, u=2)
+            for rl in range(2 * pair, 2 * pair + 2):
+                r = 4 * half + rl
+                tp = ps_sh.tile([P, 4, P], F32, tag="sh", name="tpx")
                 for k in range(4):
                     nc.tensor.transpose(
-                        out=tp[:, k, :], in_=xw[:, rl * 512 + k * P: rl * 512 + (k + 1) * P], identity=ident[:]
+                        out=tp[:, k, :], in_=xw[:, r * 512 + k * P: r * 512 + (k + 1) * P], identity=ident[:]
                     )
-                copy_on(X_EVAC[rl], gv[:, rl], tp[:].rearrange("p (g u) b -> p g b u", u=2))
+                copy_on(X_EVAC[rl], gv[:, r], tp[:].rearrange("p (g u) b -> p g b u", u=2))
+
+        def fe_quant(i):
+            t, half = divmod(i, 2)
             nc.vector.quantize_mx(
-                out=xc[:, 8 * half:8 * half + 8, :].rearrange("p a b -> p (a b)").bitcast(FP8X4),
-                scales=xs[:, 8 * half:8 * half + 8, :].rearrange("p a b -> p (a b)"),
-                in_=grp[:],
+                out=fe["xc%d" % t][:, 8 * half:8 * half + 8, :].rearrange("p a b -> p (a b)").bitcast(FP8X4),
+                scales=fe["xs%d" % t][:, 8 * half:8 * half + 8, :].rearrange("p a b -> p (a b)"),
+                in_=fe["g%d" % t][:, half * 4096:(half + 1) * 4096],
             )
 
-        def mx_half(xc, xs, u, j, half):
-            for jr in range(2 * half, 2 * half + 2):
-                ups = ps_u.tile([P, 512], F32, tag="ups", name="ups")
-                for rr in range(2):
-                    r = 2 * jr + rr
-                    for g in range(2):
-                        nc.tensor.matmul_mx(
-                            out=ups[:, rr * 256:(rr + 1) * 256],
-                            lhsT=xc[:, 2 * r + g, :].bitcast(FP8X4),
-                            lhsT_scale=xs[:, 2 * r + g, :],
-                            rhs=wc[:, r, g * 256:(g + 1) * 256].bitcast(FP8X4),
-                            rhs_scale=ws[:, r, g * 256:(g + 1) * 256],
-                            start=(g == 0),
-                            stop=(g == 1),
-                        )
-                nc.scalar.copy(out=u[:, j * 2048 + jr * 512: j * 2048 + (jr + 1) * 512], in_=ups[:])
+        def fe_mx(i, pair):
+            t, half = divmod(i, 2)
+            q, j = divmod(t, 2)
+            xc = fe["xc%d" % t]
+            xs = fe["xs%d" % t]
+            u = st[q]["u"]
+            jr = 2 * half + pair
+            ups = ps_sh.tile([P, 512], F32, tag="sh", name="ups")
+            for rr in range(2):
+                r = 2 * jr + rr
+                for g in range(2):
+                    nc.tensor.matmul_mx(
+                        out=ups[:, rr * 256:(rr + 1) * 256],
+                        lhsT=xc[:, 2 * r + g, :].bitcast(FP8X4),
+                        lhsT_scale=xs[:, 2 * r + g, :],
+                        rhs=wc[:, r, g * 256:(g + 1) * 256].bitcast(FP8X4),
+                        rhs_scale=ws[:, r, g * 256:(g + 1) * 256],
+                        start=(g == 0),
+                        stop=(g == 1),
+                    )
+            nc.scalar.copy(out=u[:, j * 2048 + jr * 512: j * 2048 + (jr + 1) * 512], in_=ups[:])
 
-        st = [dict() for q in range(NU)]
-
-        def front_unit(q):
-            u = u_pool.tile([P, 4096], F32, tag="u", name="u")
-            st[q]["u"] = u
-            for j in range(2):
-                t = 2 * q + j
-                xc = xq_pool.tile([P, 16, P], U32, tag="xc", name="xc", align_bytes=64)
-                xs = xq_pool.tile([P, 16, P], U8, tag="xs", name="xs", align_bytes=64)
-                if t == 0:
-                    w0 = load_w(0)
-                    x0 = load_x(0, 0)
-                    w1 = load_w(1)
-                    prep_w(0, w0)
-                    prep_x(x0, xc, xs, 0)
-                    w2 = load_w(2)
-                    prep_w(1, w1)
-                    mx_half(xc, xs, u, j, 0)
-                    x1 = load_x(0, 1)
-                    w3 = load_w(3)
-                    prep_w(2, w2)
-                    prep_x(x1, xc, xs, 1)
-                    prep_w(3, w3)
-                    mx_half(xc, xs, u, j, 1)
-                else:
-                    for half in range(2):
-                        xin = load_x(t, half)
-                        prep_x(xin, xc, xs, half)
-                        mx_half(xc, xs, u, j, half)
+        def fe_step(i):
+            t, half = divmod(i, 2)
+            if i < 16 and half == 0:
+                if t + 1 < 8:
+                    load_x(t + 1)
+                fe["g%d" % t] = big.tile([P, 8192], BF16, tag="big", name="grpx", align_bytes=64)
+                fe["xc%d" % t] = xq_pool.tile([P, 16, P], U32, tag="xc", name="xc", align_bytes=64)
+                fe["xs%d" % t] = xq_pool.tile([P, 16, P], U8, tag="xs", name="xs", align_bytes=64)
+                if t % 2 == 0:
+                    st[t // 2]["u"] = u_pool.tile([P, 4096], F32, tag="u", name="u")
+            for pair in range(2):
+                if i < 16:
+                    fe_transposes(i, pair)
+                if i > 0:
+                    fe_mx(i - 1, pair)
+            if i < 16:
+                fe_quant(i)
 
         def acc_transposes(dst, srcs):
             n = len(srcs)
             for i in range(n):
                 nc.tensor.matmul(
-                    out=dst, lhsT=srcs[i], rhs=ident[:], is_transpose=(i % 8 != 3), start=(i == 0), stop=(i == n - 1)
+                    out=dst, lhsT=srcs[i], rhs=ident[:],
+                    is_transpose=(REG_EVERY == 0 or i % REG_EVERY != REG_EVERY - 1),
+                    start=(i == 0), stop=(i == n - 1),
                 )
 
-        def reduce_routes(src, scale):
-            if PE_RED:
-                sv = src[:].rearrange("p (j r h k) -> p j r h k", j=2, r=8, h=2)
-                acc = ps_acc.tile([P, 2, 2, P], F32, tag="acc", name="acc_s")
-                for j in range(2):
-                    for h in range(2):
-                        acc_transposes(acc[:, j, h, :], [sv[:, j, r, h, :] for r in range(8)])
-                s_t = sm.tile([P, 2, 2, P], F32, tag="s_t", name="s_t")
-                for h in range(2):
-                    nc.scalar.activation(
-                        out=s_t[:, :, h, :], in_=acc[:, :, h, :], func=ACT.Identity,
-                        bias=bias_t[:, h:h + 1], scale=scale,
-                    )
-                back = ps_back.tile([P, 512], F32, tag="back", name="back_s")
-                for j in range(2):
-                    for h in range(2):
-                        nc.tensor.transpose(
-                            out=back[:, (2 * j + h) * P:(2 * j + h + 1) * P], in_=s_t[:, j, h, :], identity=ident[:]
-                        )
-                return back
-            red = sm.tile([P, 512], F32, tag="red", name="red")
-            s_sb = sm.tile([P, 512], F32, tag="s_sb", name="s_sb")
-            for j in range(2):
-                nc.vector.tensor_reduce(
-                    out=red[:, j * 256:(j + 1) * 256],
-                    in_=src[:, j * 2048:(j + 1) * 2048].rearrange("p (r k) -> p k r", r=8),
-                    axis=AX.X, op=ALU.add,
-                )
-                nc.vector.scalar_tensor_tensor(
-                    out=s_sb[:, j * 256:(j + 1) * 256], in0=red[:, j * 256:(j + 1) * 256], scalar=scale,
-                    in1=bc[:], op0=ALU.mult, op1=ALU.add,
-                )
-            return s_sb
-
-        def squash_gain(s):
-            sq = sm.tile([P, 512], F32, tag="sq", name="sq")
-            nc.scalar.activation(out=sq[:], in_=s[:], func=ACT.Square)
-            n2 = sm.tile([P, 32], F32, tag="n2", name="n2")
-            nc.vector.tensor_reduce(
-                out=n2[:].rearrange("p (j c) -> p j c", j=2),
-                in_=sq[:].rearrange("p (j o c) -> p j c o", j=2, c=16),
-                axis=AX.X, op=ALU.add,
-            )
-            nn = sm.tile([P, 32], F32, tag="nn", name="nn")
-            nc.scalar.activation(out=nn[:], in_=n2[:], func=ACT.Sqrt, bias=tinyb[:, 0:1])
-            dd = sm.tile([P, 32], F32, tag="dd", name="dd")
-            nc.vector.tensor_scalar(out=dd[:], in0=n2[:], scalar1=1.0 + EPS, scalar2=None, op0=ALU.add)
-            rd = sm.tile([P, 32], F32, tag="rd", name="rd")
-            nc.vector.reciprocal(out=rd[:], in_=dd[:])
-            gain = keep.tile([P, 32], F32, tag="gain", name="gain")
-            nc.vector.tensor_mul(out=gain[:], in0=nn[:], in1=rd[:])
-            return gain
-
-        def stage_s(q, k):
-            u = st[q]["u"]
-            if k == 0:
-                s = reduce_routes(u, 1.0 / 16.0)
-            else:
-                cc = st[q]["c"]
-                ps = p_pool.tile([P, 4096], F32, tag="p", name="p_s")
-                pv = ps[:].rearrange("p (a h o c) -> p a h o c", a=16, h=2, c=16)
-                uv = u[:].rearrange("p (a h o c) -> p a h o c", a=16, h=2, c=16)
-                cv = cc[:].rearrange("p (a c) -> p a c", c=16)
-                for j in range(2):
-                    for h in range(2):
-                        eng = nc.gpsimd if S_MULT_ENG[2 * j + h] == "G" else nc.vector
-                        eng.tensor_tensor(
-                            out=pv[:, 8 * j:8 * j + 8, h],
-                            in0=uv[:, 8 * j:8 * j + 8, h],
-                            in1=cv[:, 8 * j:8 * j + 8, :].unsqueeze(2).to_broadcast([P, 8, 8, 16]),
-                            op=ALU.mult,
-                        )
-                s = reduce_routes(ps, 1.0)
-            st[q]["s"] = s
-            gain = squash_gain(s)
-            st[q]["gain"] = gain
-            if k == 2:
-                vo = sm.tile([P, 512], F32, tag="vo", name="vo")
-                nc.vector.tensor_tensor(
-                    out=vo[:].rearrange("p (j c o) -> p j c o", j=2, o=16),
-                    in0=s[:].rearrange("p (j o c) -> p j c o", j=2, c=16),
-                    in1=gain[:].rearrange("p (j c) -> p j c", j=2).unsqueeze(3).to_broadcast([P, 2, 16, 16]),
+        def s_mult(q, j):
+            d = st[q]
+            if j == 0:
+                d["p"] = big.tile([P, 4096], F32, tag="big", name="p_s", align_bytes=64)
+            pv = d["p"][:].rearrange("p (a h o c) -> p a h o c", a=16, h=2, c=16)
+            uv = d["u"][:].rearrange("p (a h o c) -> p a h o c", a=16, h=2, c=16)
+            cv = d["td"][:].rearrange("p (a c) -> p a c", c=16)
+            for h in range(2):
+                eng = nc.gpsimd if S_MULT[2 * j + h] == "G" else nc.vector
+                eng.tensor_tensor(
+                    out=pv[:, 8 * j:8 * j + 8, h],
+                    in0=uv[:, 8 * j:8 * j + 8, h],
+                    in1=cv[:, 8 * j:8 * j + 8, :].unsqueeze(2).to_broadcast([P, 8, 8, 16]),
                     op=ALU.mult,
                 )
-                nc.sync.dma_start(
-                    out=out[q * 256:(q + 1) * 256].rearrange("(j b) c o -> b j (c o)", j=2),
-                    in_=vo[:].rearrange("p (j k) -> p j k", j=2),
+
+        def s_acc(q, k, j):
+            d = st[q]
+            src = d["u"] if k == 0 else d["p"]
+            sv = src[:].rearrange("p (j r h k) -> p j r h k", j=2, r=8, h=2)
+            if j == 0:
+                d["acc"] = ps_sh.tile([P, 2, 2, P], F32, tag="sh", name="acc_s")
+            for h in range(2):
+                acc_transposes(d["acc"][:, j, h, :], [sv[:, j, r, h, :] for r in range(8)])
+
+        def s_evac(q, k):
+            d = st[q]
+            d["ta"] = un.tile([P, 512], F32, tag="ta", name="ta")
+            tv = d["ta"][:].rearrange("p (j h b) -> p j h b", j=2, h=2)
+            for h in range(2):
+                nc.scalar.activation(
+                    out=tv[:, :, h, :], in_=d["acc"][:, :, h, :], func=ACT.Identity,
+                    bias=bias_t[:, h:h + 1], scale=(1.0 / 16.0 if k == 0 else 1.0),
                 )
 
-        def stage_a(q, k):
-            u = st[q]["u"]
-            s = st[q]["s"]
-            gain = st[q]["gain"]
-            pa = p_pool.tile([P, 4096], F32, tag="p", name="p_a")
-            pv = pa[:].rearrange("p (j o r c) -> p j o r c", j=2, o=16, c=16)
-            uv = u[:].rearrange("p (j r o c) -> p j o r c", j=2, r=8, c=16)
-            sv = s[:].rearrange("p (j o c) -> p j o c", j=2, c=16)
+        def s_back(q):
+            d = st[q]
+            d["s"] = ps_lg.tile([P, 512], F32, tag="lg", name="back_s")
+            for jh in range(4):
+                nc.tensor.transpose(
+                    out=d["s"][:, jh * P:(jh + 1) * P], in_=d["ta"][:, jh * P:(jh + 1) * P], identity=ident[:]
+                )
+
+        def sq_square(q):
+            d = st[q]
+            nc.scalar.activation(out=d["ta"][:], in_=d["s"][:], func=ACT.Square)
+
+        def sq_n2(q):
+            d = st[q]
+            d["n2"] = un.tile([P, 32], F32, tag="n2", name="n2")
+            nc.vector.tensor_reduce(
+                out=d["n2"][:].rearrange("p (j c) -> p j c", j=2),
+                in_=d["ta"][:].rearrange("p (j o c) -> p j c o", j=2, c=16),
+                axis=AX.X, op=ALU.add,
+            )
+            d["rd"] = un.tile([P, 32], F32, tag="rd", name="rd")
+            nc.vector.tensor_scalar(out=d["rd"][:], in0=d["n2"][:], scalar1=1.0 + EPS, scalar2=None, op0=ALU.add)
+            nc.vector.reciprocal(out=d["rd"][:], in_=d["rd"][:])
+
+        def sq_sqrt(q):
+            d = st[q]
+            d["nn"] = un.tile([P, 32], F32, tag="nn", name="nn")
+            nc.scalar.activation(out=d["nn"][:], in_=d["n2"][:], func=ACT.Sqrt, bias=tinyb[:, 0:1])
+
+        def sq_gain(q):
+            d = st[q]
+            d["gain"] = un.tile([P, 32], F32, tag="gain", name="gain")
+            nc.vector.tensor_mul(out=d["gain"][:], in0=d["nn"][:], in1=d["rd"][:])
+
+        def a_mult(q, j):
+            d = st[q]
+            if j == 0:
+                d["pa"] = big.tile([P, 4096], F32, tag="big", name="p_a", align_bytes=64)
+            pv = d["pa"][:].rearrange("p (j o r c) -> p j o r c", j=2, o=16, c=16)
+            uv = d["u"][:].rearrange("p (j r o c) -> p j o r c", j=2, r=8, c=16)
+            sv = d["s"][:].rearrange("p (j o c) -> p j o c", j=2, c=16)
+            for oh in range(2):
+                nc.vector.tensor_tensor(
+                    out=pv[:, j, 8 * oh:8 * oh + 8],
+                    in0=uv[:, j, 8 * oh:8 * oh + 8],
+                    in1=sv[:, j, 8 * oh:8 * oh + 8, :].unsqueeze(2).to_broadcast([P, 8, 8, 16]),
+                    op=ALU.mult,
+                )
+
+        def a_acc(q, j):
+            d = st[q]
+            pk = d["pa"][:].rearrange("p (j o k) -> p j o k", j=2, o=16)
+            if j == 0:
+                d["acca"] = ps_sh.tile([P, 2, P], F32, tag="sh", name="acc_a")
+            acc_transposes(d["acca"][:, j, :], [pk[:, j, o, :] for o in range(16)])
+
+        def a_evac(q):
+            d = st[q]
+            d["tb"] = un.tile([P, 256], F32, tag="tb", name="tb")
+            nc.scalar.copy(out=d["tb"][:].rearrange("p (j b) -> p j b", j=2), in_=d["acca"][:])
+
+        def a_back(q):
+            d = st[q]
+            d["araw"] = ps_sh.tile([P, 256], F32, tag="sh", name="back_a")
             for j in range(2):
-                for oh in range(2):
-                    nc.vector.tensor_tensor(
-                        out=pv[:, j, 8 * oh:8 * oh + 8],
-                        in0=uv[:, j, 8 * oh:8 * oh + 8],
-                        in1=sv[:, j, 8 * oh:8 * oh + 8, :].unsqueeze(2).to_broadcast([P, 8, 8, 16]),
-                        op=ALU.mult,
-                    )
-            if PE_RED:
-                pk = pa[:].rearrange("p (j o k) -> p j o k", j=2, o=16)
-                acc = ps_acc.tile([P, 2, P], F32, tag="acc", name="acc_a")
-                for j in range(2):
-                    acc_transposes(acc[:, j, :], [pk[:, j, o, :] for o in range(16)])
-                a_t = sm.tile([P, 2, P], F32, tag="a_t", name="a_t")
-                nc.scalar.copy(out=a_t[:], in_=acc[:])
-                araw = ps_back.tile([P, 256], F32, tag="back", name="back_a")
-                for j in range(2):
-                    nc.tensor.transpose(out=araw[:, j * P:(j + 1) * P], in_=a_t[:, j, :], identity=ident[:])
-            else:
-                araw = sm.tile([P, 256], F32, tag="a_sb", name="a_sb")
-                for j in range(2):
-                    nc.vector.tensor_reduce(
-                        out=araw[:, j * P:(j + 1) * P],
-                        in_=pa[:, j * 2048:(j + 1) * 2048].rearrange("p (o k) -> p k o", o=16),
-                        axis=AX.X, op=ALU.add,
-                    )
-            gv = gain[:].rearrange("p (j c) -> p j c", j=2).unsqueeze(2).to_broadcast([P, 2, 8, 16])
-            logit = keep.tile([P, 256], F32, tag="logit%d" % k, name="logit")
-            if k == 0:
-                nc.vector.tensor_tensor(
-                    out=logit[:].rearrange("p (j r c) -> p j r c", j=2, c=16),
-                    in0=araw[:].rearrange("p (j r c) -> p j r c", j=2, c=16), in1=gv, op=ALU.mult,
+                nc.tensor.transpose(
+                    out=d["araw"][:, j * P:(j + 1) * P], in_=d["tb"][:, j * P:(j + 1) * P], identity=ident[:]
                 )
-            else:
-                tmp = sm.tile([P, 256], F32, tag="tmp", name="tmp")
-                nc.vector.tensor_tensor(
-                    out=tmp[:].rearrange("p (j r c) -> p j r c", j=2, c=16),
-                    in0=araw[:].rearrange("p (j r c) -> p j r c", j=2, c=16), in1=gv, op=ALU.mult,
-                )
-                nc.vector.tensor_add(out=logit[:], in0=tmp[:], in1=st[q]["logit"][:])
-            st[q]["logit"] = logit
-            lv = logit[:].rearrange("p (a c) -> p a c", c=16)
-            nmax = sm.tile([P, 16], F32, tag="nmax", name="nmax")
-            nc.vector.tensor_reduce(out=nmax[:], in_=lv, axis=AX.X, op=ALU.max)
-            sh = sm.tile([P, 256], F32, tag="sh", name="sh")
-            nc.vector.tensor_tensor(
-                out=sh[:].rearrange("p (a c) -> p a c", c=16), in0=lv,
-                in1=nmax[:].unsqueeze(2).to_broadcast([P, 16, 16]), op=ALU.subtract,
-            )
-            ex = sm.tile([P, 256], F32, tag="ex", name="ex")
-            nc.scalar.activation(out=ex[:], in_=sh[:], func=ACT.Exp)
-            ev = ex[:].rearrange("p (a c) -> p a c", c=16)
-            esum = sm.tile([P, 16], F32, tag="esum", name="esum")
-            nc.vector.tensor_reduce(out=esum[:], in_=ev, axis=AX.X, op=ALU.add)
-            rs = sm.tile([P, 16], F32, tag="rs", name="rs")
-            nc.vector.reciprocal(out=rs[:], in_=esum[:])
-            cc = keep.tile([P, 256], F32, tag="cc", name="cc")
-            nc.vector.tensor_tensor(
-                out=cc[:].rearrange("p (a c) -> p a c", c=16), in0=ev,
-                in1=rs[:].unsqueeze(2).to_broadcast([P, 16, 16]), op=ALU.mult,
-            )
-            st[q]["c"] = cc
 
-        for slot in range(NU + 3):
-            if slot < NU:
-                front_unit(slot)
-            if 0 <= slot - 1 < NU:
-                stage_s(slot - 1, 0)
-                stage_a(slot - 1, 0)
-            if 0 <= slot - 2 < NU:
-                stage_s(slot - 2, 1)
-                stage_a(slot - 2, 1)
-            if 0 <= slot - 3 < NU:
-                stage_s(slot - 3, 2)
+        def a_logit(q, k):
+            d = st[q]
+            gv = d["gain"][:].rearrange("p (j c) -> p j c", j=2).unsqueeze(2).to_broadcast([P, 2, 8, 16])
+            av = d["araw"][:].rearrange("p (j r c) -> p j r c", j=2, c=16)
+            if k == 0:
+                d["logit"] = un.tile([P, 256], F32, tag="logit", name="logit")
+                nc.vector.tensor_tensor(
+                    out=d["logit"][:].rearrange("p (j r c) -> p j r c", j=2, c=16), in0=av, in1=gv, op=ALU.mult
+                )
+            else:
+                nc.vector.tensor_tensor(
+                    out=d["tb"][:].rearrange("p (j r c) -> p j r c", j=2, c=16), in0=av, in1=gv, op=ALU.mult
+                )
+                nc.vector.tensor_add(out=d["logit"][:], in0=d["tb"][:], in1=d["logit"][:])
+            lv = d["logit"][:].rearrange("p (a c) -> p a c", c=16)
+            d["mx"] = un.tile([P, 16], F32, tag="mx", name="mx")
+            nc.vector.tensor_reduce(out=d["mx"][:], in_=lv, axis=AX.X, op=ALU.max)
+            d["td"] = un.tile([P, 256], F32, tag="td", name="td")
+            nc.vector.tensor_tensor(
+                out=d["td"][:].rearrange("p (a c) -> p a c", c=16), in0=lv,
+                in1=d["mx"][:].unsqueeze(2).to_broadcast([P, 16, 16]), op=ALU.subtract,
+            )
+
+        def a_exp(q):
+            d = st[q]
+            nc.scalar.activation(out=d["td"][:], in_=d["td"][:], func=ACT.Exp)
+
+        def a_soft(q):
+            d = st[q]
+            ev = d["td"][:].rearrange("p (a c) -> p a c", c=16)
+            nc.vector.tensor_reduce(out=d["mx"][:], in_=ev, axis=AX.X, op=ALU.add)
+            nc.vector.reciprocal(out=d["mx"][:], in_=d["mx"][:])
+            nc.vector.tensor_tensor(
+                out=ev, in0=ev, in1=d["mx"][:].unsqueeze(2).to_broadcast([P, 16, 16]), op=ALU.mult
+            )
+
+        def out_v(q):
+            d = st[q]
+            nc.vector.tensor_tensor(
+                out=d["ta"][:].rearrange("p (j c o) -> p j c o", j=2, o=16),
+                in0=d["s"][:].rearrange("p (j o c) -> p j c o", j=2, c=16),
+                in1=d["gain"][:].rearrange("p (j c) -> p j c", j=2).unsqueeze(3).to_broadcast([P, 2, 16, 16]),
+                op=ALU.mult,
+            )
+            nc.sync.dma_start(
+                out=out[q * 256:(q + 1) * 256].rearrange("(j b) c o -> b j (c o)", j=2),
+                in_=d["ta"][:].rearrange("p (j k) -> p j k", j=2),
+            )
+
+        def routing_steps(q):
+            steps = []
+            for k in range(3):
+                if k > 0:
+                    steps.append(lambda: s_mult(q, 0))
+                    steps.append(lambda: s_mult(q, 1))
+                steps.append(lambda k=k: s_acc(q, k, 0))
+                steps.append(lambda k=k: s_acc(q, k, 1))
+                steps.append(lambda k=k: s_evac(q, k))
+                steps.append(lambda: s_back(q))
+                steps.append(lambda: sq_square(q))
+                if k < 2:
+                    steps.append(lambda: a_mult(q, 0))
+                    steps.append(lambda: sq_n2(q))
+                    steps.append(lambda: a_mult(q, 1))
+                    steps.append(lambda: a_acc(q, 0))
+                    steps.append(lambda: sq_sqrt(q))
+                    steps.append(lambda: a_acc(q, 1))
+                    steps.append(lambda: sq_gain(q))
+                    steps.append(lambda: a_evac(q))
+                    steps.append(lambda: a_back(q))
+                    steps.append(lambda k=k: a_logit(q, k))
+                    steps.append(lambda: a_exp(q))
+                    steps.append(lambda: a_soft(q))
+                else:
+                    steps.append(lambda: sq_n2(q))
+                    steps.append(lambda: sq_sqrt(q))
+                    steps.append(lambda: sq_gain(q))
+                    steps.append(lambda: out_v(q))
+            return steps
+
+        chains = []
+
+        def advance(n):
+            for rep in range(n):
+                for ch in chains:
+                    if ch[1] < len(ch[0]):
+                        ch[0][ch[1]]()
+                        ch[1] = ch[1] + 1
+
+        load_w(0)
+        load_x(0)
+        load_w(1)
+        w_step(0)
+        w_step(1)
+        fe_step(0)
+        w_step(2)
+        w_step(3)
+        for i in range(1, 17):
+            fe_step(i)
+            if i % 4 == 0:
+                chains.append([routing_steps(i // 4 - 1), 0])
+            advance(RATE)
+        for rep in range(60):
+            advance(1)

@@ -23,7 +23,7 @@ RATE = 3
 X_EVAC = "SSSV"
 W_EVAC = "SV"
 S_MULT = "GGGG"
-REG_EVERY = 0
+REG_EVERY = 7
 SH_BUFS = 5
 LG_BUFS = 3
 BIG_BUFS = 6
@@ -178,14 +178,20 @@ def tile_capsulelayer_t_kernel(tc, x, W, bias, out):
             if i < 16:
                 fe_quant(i)
 
+        count = [0]
+
+        def turn(dst, src, first, last):
+            count[0] = count[0] + 1
+            nc.tensor.matmul(
+                out=dst, lhsT=src, rhs=ident[:],
+                is_transpose=(REG_EVERY == 0 or count[0] % REG_EVERY != 0),
+                start=first, stop=last,
+            )
+
         def acc_transposes(dst, srcs):
             n = len(srcs)
             for i in range(n):
-                nc.tensor.matmul(
-                    out=dst, lhsT=srcs[i], rhs=ident[:],
-                    is_transpose=(REG_EVERY == 0 or i % REG_EVERY != REG_EVERY - 1),
-                    start=(i == 0), stop=(i == n - 1),
-                )
+                turn(dst, srcs[i], i == 0, i == n - 1)
 
         def s_mult(q, j):
             d = st[q]
@@ -226,9 +232,7 @@ def tile_capsulelayer_t_kernel(tc, x, W, bias, out):
             d = st[q]
             d["s"] = ps_lg.tile([P, 512], F32, tag="lg", name="back_s")
             for jh in range(4):
-                nc.tensor.transpose(
-                    out=d["s"][:, jh * P:(jh + 1) * P], in_=d["ta"][:, jh * P:(jh + 1) * P], identity=ident[:]
-                )
+                turn(d["s"][:, jh * P:(jh + 1) * P], d["ta"][:, jh * P:(jh + 1) * P], True, True)
 
         def sq_square(q):
             d = st[q]
@@ -287,9 +291,7 @@ def tile_capsulelayer_t_kernel(tc, x, W, bias, out):
             d = st[q]
             d["araw"] = ps_sh.tile([P, 256], F32, tag="sh", name="back_a")
             for j in range(2):
-                nc.tensor.transpose(
-                    out=d["araw"][:, j * P:(j + 1) * P], in_=d["tb"][:, j * P:(j + 1) * P], identity=ident[:]
-                )
+                turn(d["araw"][:, j * P:(j + 1) * P], d["tb"][:, j * P:(j + 1) * P], True, True)
 
         def a_logit(q, k):
             d = st[q]

@@ -22,8 +22,8 @@ MANUAL = False
 RATE = 3
 X_EVAC = "SSSV"
 W_EVAC = "SV"
-S_MULT = "GGGG"
-REG_EVERY = 7
+S_MULT = "VVVV"
+REG_EVERY = 0
 SH_BUFS = 5
 LG_BUFS = 3
 BIG_BUFS = 6

@@ -19,14 +19,15 @@ NU = 4
 EPS = 1e-8
 
 MANUAL = False
-RATE = 3
-X_EVAC = "SSSV"
-W_EVAC = "SV"
-S_MULT = "VVVV"
+RATE = 1
+X_EVAC = "SSSS"
+W_EVAC = "SS"
+S_MULT = "GVGV"
 REG_EVERY = 0
 SH_BUFS = 5
 LG_BUFS = 3
 BIG_BUFS = 6
+A_RED_V = ()
 
 
 def tile_capsulelayer_t_kernel(tc, x, W, bias, out):
@@ -159,6 +160,12 @@ def tile_capsulelayer_t_kernel(tc, x, W, bias, out):
                         stop=(g == 1),
                     )
             nc.scalar.copy(out=u[:, j * 2048 + jr * 512: j * 2048 + (jr + 1) * 512], in_=ups[:])
+            s1 = st[q]["s"]
+            for rr in range(2):
+                nc.vector.scalar_tensor_tensor(
+                    out=s1[:, j * 256:(j + 1) * 256], in0=ups[:, rr * 256:(rr + 1) * 256], scalar=1.0 / 16.0,
+                    in1=(bc[:] if 2 * jr + rr == 0 else s1[:, j * 256:(j + 1) * 256]), op0=ALU.mult, op1=ALU.add,
+                )
 
         def fe_step(i):
             t, half = divmod(i, 2)
@@ -170,6 +177,7 @@ def tile_capsulelayer_t_kernel(tc, x, W, bias, out):
                 fe["xs%d" % t] = xq_pool.tile([P, 16, P], U8, tag="xs", name="xs", align_bytes=64)
                 if t % 2 == 0:
                     st[t // 2]["u"] = u_pool.tile([P, 4096], F32, tag="u", name="u")
+                    st[t // 2]["s"] = un.tile([P, 512], F32, tag="s1", name="s1")
             for pair in range(2):
                 if i < 16:
                     fe_transposes(i, pair)
@@ -234,8 +242,10 @@ def tile_capsulelayer_t_kernel(tc, x, W, bias, out):
             for jh in range(4):
                 turn(d["s"][:, jh * P:(jh + 1) * P], d["ta"][:, jh * P:(jh + 1) * P], True, True)
 
-        def sq_square(q):
+        def sq_square(q, k):
             d = st[q]
+            if k == 0:
+                d["ta"] = un.tile([P, 512], F32, tag="ta", name="ta")
             nc.scalar.activation(out=d["ta"][:], in_=d["s"][:], func=ACT.Square)
 
         def sq_n2(q):
@@ -275,8 +285,17 @@ def tile_capsulelayer_t_kernel(tc, x, W, bias, out):
                     op=ALU.mult,
                 )
 
-        def a_acc(q, j):
+        def a_acc(q, k, j):
             d = st[q]
+            if k in A_RED_V:
+                if j == 0:
+                    d["araw"] = un.tile([P, 256], F32, tag="tb", name="araw_sb")
+                nc.vector.tensor_reduce(
+                    out=d["araw"][:, j * P:(j + 1) * P],
+                    in_=d["pa"][:, j * 2048:(j + 1) * 2048].rearrange("p (o k) -> p k o", o=16),
+                    axis=AX.X, op=ALU.add,
+                )
+                return
             pk = d["pa"][:].rearrange("p (j o k) -> p j o k", j=2, o=16)
             if j == 0:
                 d["acca"] = ps_sh.tile([P, 2, P], F32, tag="sh", name="acc_a")
@@ -303,10 +322,11 @@ def tile_capsulelayer_t_kernel(tc, x, W, bias, out):
                     out=d["logit"][:].rearrange("p (j r c) -> p j r c", j=2, c=16), in0=av, in1=gv, op=ALU.mult
                 )
             else:
+                tmp = d["araw"] if k in A_RED_V else d["tb"]
                 nc.vector.tensor_tensor(
-                    out=d["tb"][:].rearrange("p (j r c) -> p j r c", j=2, c=16), in0=av, in1=gv, op=ALU.mult
+                    out=tmp[:].rearrange("p (j r c) -> p j r c", j=2, c=16), in0=av, in1=gv, op=ALU.mult
                 )
-                nc.vector.tensor_add(out=d["logit"][:], in0=d["tb"][:], in1=d["logit"][:])
+                nc.vector.tensor_add(out=d["logit"][:], in0=tmp[:], in1=d["logit"][:])
             lv = d["logit"][:].rearrange("p (a c) -> p a c", c=16)
             d["mx"] = un.tile([P, 16], F32, tag="mx", name="mx")
             nc.vector.tensor_reduce(out=d["mx"][:], in_=lv, axis=AX.X, op=ALU.max)
@@ -348,21 +368,22 @@ def tile_capsulelayer_t_kernel(tc, x, W, bias, out):
                 if k > 0:
                     steps.append(lambda: s_mult(q, 0))
                     steps.append(lambda: s_mult(q, 1))
-                steps.append(lambda k=k: s_acc(q, k, 0))
-                steps.append(lambda k=k: s_acc(q, k, 1))
-                steps.append(lambda k=k: s_evac(q, k))
-                steps.append(lambda: s_back(q))
-                steps.append(lambda: sq_square(q))
+                    steps.append(lambda k=k: s_acc(q, k, 0))
+                    steps.append(lambda k=k: s_acc(q, k, 1))
+                    steps.append(lambda k=k: s_evac(q, k))
+                    steps.append(lambda: s_back(q))
+                steps.append(lambda k=k: sq_square(q, k))
                 if k < 2:
                     steps.append(lambda: a_mult(q, 0))
                     steps.append(lambda: sq_n2(q))
                     steps.append(lambda: a_mult(q, 1))
-                    steps.append(lambda: a_acc(q, 0))
+                    steps.append(lambda k=k: a_acc(q, k, 0))
                     steps.append(lambda: sq_sqrt(q))
-                    steps.append(lambda: a_acc(q, 1))
+                    steps.append(lambda k=k: a_acc(q, k, 1))
                     steps.append(lambda: sq_gain(q))
-                    steps.append(lambda: a_evac(q))
-                    steps.append(lambda: a_back(q))
+                    if k not in A_RED_V:
+                        steps.append(lambda: a_evac(q))
+                        steps.append(lambda: a_back(q))
                     steps.append(lambda k=k: a_logit(q, k))
                     steps.append(lambda: a_exp(q))
                     steps.append(lambda: a_soft(q))

@@ -22,7 +22,7 @@ MANUAL = False
 RATE = 1
 X_EVAC = "SSSS"
 W_EVAC = "SS"
-S_MULT = "GVGV"
+S_MULT = "VVVV"
 REG_EVERY = 0
 SH_BUFS = 5
 LG_BUFS = 3

@@ -23,7 +23,7 @@ RATE = 1
 X_EVAC = "SSSS"
 W_EVAC = "SS"
 S_MULT = "VVVV"
-REG_EVERY = 0
+REG_EVERY = 6
 SH_BUFS = 5
 LG_BUFS = 3
 BIG_BUFS = 6
@@ -159,12 +159,21 @@ def tile_capsulelayer_t_kernel(tc, x, W, bias, out):
                         start=(g == 0),
                         stop=(g == 1),
                     )
+                    nc.tensor.matmul_mx(
+                        out=st[q]["sum"][:, j * 256:(j + 1) * 256],
+                        lhsT=xc[:, 2 * r + g, :].bitcast(FP8X4),
+                        lhsT_scale=xs[:, 2 * r + g, :],
+                        rhs=wc[:, r, g * 256:(g + 1) * 256].bitcast(FP8X4),
+                        rhs_scale=ws[:, r, g * 256:(g + 1) * 256],
+                        start=(r == 0 and g == 0),
+                        stop=(r == 7 and g == 1),
+                    )
             nc.scalar.copy(out=u[:, j * 2048 + jr * 512: j * 2048 + (jr + 1) * 512], in_=ups[:])
-            s1 = st[q]["s"]
-            for rr in range(2):
+            if j == 1 and jr == 3:
                 nc.vector.scalar_tensor_tensor(
-                    out=s1[:, j * 256:(j + 1) * 256], in0=ups[:, rr * 256:(rr + 1) * 256], scalar=1.0 / 16.0,
-                    in1=(bc[:] if 2 * jr + rr == 0 else s1[:, j * 256:(j + 1) * 256]), op0=ALU.mult, op1=ALU.add,
+                    out=st[q]["s"][:].rearrange("p (j k) -> p j k", j=2),
+                    in0=st[q]["sum"][:].rearrange("p (j k) -> p j k", j=2), scalar=1.0 / 16.0,
+                    in1=bc[:].unsqueeze(1).to_broadcast([P, 2, 256]), op0=ALU.mult, op1=ALU.add,
                 )
 
         def fe_step(i):
@@ -178,6 +187,7 @@ def tile_capsulelayer_t_kernel(tc, x, W, bias, out):
                 if t % 2 == 0:
                     st[t // 2]["u"] = u_pool.tile([P, 4096], F32, tag="u", name="u")
                     st[t // 2]["s"] = un.tile([P, 512], F32, tag="s1", name="s1")
+                    st[t // 2]["sum"] = ps_lg.tile([P, 512], F32, tag="lg", name="sum1")
             for pair in range(2):
                 if i < 16:
                     fe_transposes(i, pair)

from contextlib import ExitStack

import concourse.mybir as mybir
from concourse.masks import make_identity

F32 = mybir.dt.float32
BF16 = mybir.dt.bfloat16
U32 = mybir.dt.uint32
U8 = mybir.dt.uint8
FP8X4 = mybir.dt.float8_e4m3fn_x4
ALU = mybir.AluOpType
ACT = mybir.ActivationFunctionType
AX = mybir.AxisListType

FLOPS = 2 * 1024 * 8 * 256 * 1024

P = 128
NU = 4
EPS = 1e-8

MANUAL = False
RATE = 1
X_EVAC = "SSSS"
W_EVAC = "SS"
S_MULT = "VVVV"
REG_EVERY = 6
SH_BUFS = 5
LG_BUFS = 3
BIG_BUFS = 6
A_RED_V = ()


def tile_capsulelayer_t_kernel(tc, x, W, bias, out):
    nc = tc.nc
    with ExitStack() as ctx:
        const = ctx.enter_context(tc.tile_pool(name="const", bufs=1))
        big = ctx.enter_context(tc.tile_pool(name="big", bufs=BIG_BUFS))
        xq_pool = ctx.enter_context(tc.tile_pool(name="xq", bufs=2))
        u_pool = ctx.enter_context(tc.tile_pool(name="u", bufs=4))
        un = ctx.enter_context(tc.tile_pool(name="un", bufs=4))
        ps_sh = ctx.enter_context(tc.psum_pool(name="pssh", bufs=SH_BUFS))
        ps_lg = ctx.enter_context(tc.psum_pool(name="pslg", bufs=LG_BUFS))

        def copy_on(letter, dst, src):
            if letter == "S":
                nc.scalar.copy(out=dst, in_=src)
            else:
                nc.vector.tensor_copy(out=dst, in_=src)

        ident = const.tile([P, P], F32, name="ident")
        make_identity(nc, ident[:])
        tinyb = const.tile([P, 1], F32, name="tinyb")
        nc.vector.memset(tinyb[:], 1e-30)
        braw = const.tile([P, 256], BF16, name="braw")
        nc.sync.dma_start(out=braw[:], in_=bias.rearrange("a b c o -> (a b c o)").partition_broadcast(P))
        bc = const.tile([P, 256], F32, name="bc")
        nc.vector.tensor_copy(
            out=bc[:].rearrange("p (o c) -> p o c", c=16),
            in_=braw[:].rearrange("p (c o) -> p o c", o=16),
        )
        wc = const.tile([P, 8, 512], U32, name="wc", align_bytes=64)
        ws = const.tile([P, 8, 512], U8, name="ws", align_bytes=64)
        bias_t = const.tile([P, 2], F32, name="bias_t")
        tpb = ps_sh.tile([P, 4, P], F32, tag="sh", name="tpb")
        for h in range(2):
            nc.tensor.transpose(out=tpb[:, h, :], in_=bc[:, h * P:(h + 1) * P], identity=ident[:])
        for h in range(2):
            nc.vector.tensor_copy(out=bias_t[:, h:h + 1], in_=tpb[:, h, 0:1])

        if MANUAL:
            ctx.enter_context(tc.manual_schedule())

        w_rows = W.rearrange("r c o i -> (r c o) i")
        fe = dict()
        st = [dict() for q in range(NU)]

        def load_w(wt):
            win = big.tile([P, 8192], BF16, tag="big", name="win", align_bytes=64)
            nc.sync.dma_start(
                out=win[:].rearrange("p (t i) -> p t i", t=8),
                in_=w_rows[wt * 1024:(wt + 1) * 1024, :].rearrange("(t p) i -> p t i", p=P),
            )
            fe["w%d" % wt] = win

        def w_step(wq):
            wt, sub = divmod(wq, 2)
            if sub == 0:
                fe["gw%d" % wt] = big.tile([P, 8192], BF16, tag="big", name="grpw", align_bytes=64)
            ww = fe["w%d" % wt][:].bitcast(F32)
            grp = fe["gw%d" % wt]
            gv = grp[:].bitcast(F32).rearrange("p (r g o c u) -> p r g o c u", r=4, g=2, o=16, c=16, u=2)
            for rl in range(2 * sub, 2 * sub + 2):
                for h in range(2):
                    t = rl * 2 + h
                    tp = ps_sh.tile([P, 4, P], F32, tag="sh", name="tpw")
                    for k in range(4):
                        nc.tensor.transpose(
                            out=tp[:, k, :], in_=ww[:, t * 512 + k * P: t * 512 + (k + 1) * P], identity=ident[:]
                        )
                    for g in range(2):
                        copy_on(
                            W_EVAC[g],
                            gv[:, rl, g, :, 8 * h:8 * h + 8, :],
                            tp[:, 2 * g:2 * g + 2, :].rearrange("p u (c o) -> p o c u", o=16),
                        )
            nc.vector.quantize_mx(
                out=wc[:, 2 * wq:2 * wq + 2, :].rearrange("p a b -> p (a b)").bitcast(FP8X4),
                scales=ws[:, 2 * wq:2 * wq + 2, :].rearrange("p a b -> p (a b)"),
                in_=grp[:, sub * 4096:(sub + 1) * 4096],
            )

        def load_x(t):
            xin = big.tile([P, 8192], BF16, tag="big", name="xin", align_bytes=64)
            for half in range(2):
                nc.sync.dma_start(
                    out=xin[:, half * 4096:(half + 1) * 4096],
                    in_=x[t * P:(t + 1) * P, 4 * half:4 * half + 4, :].rearrange("b r i -> b (r i)"),
                )
            fe["x%d" % t] = xin

        def fe_transposes(i, pair):
            t, half = divmod(i, 2)
            xw = fe["x%d" % t][:].bitcast(F32)
            gv = fe["g%d" % t][:].bitcast(F32).rearrange("p (r g b u) -> p r g b u", r=8, g=2, b=P, u=2)
            for rl in range(2 * pair, 2 * pair + 2):
                r = 4 * half + rl
                tp = ps_sh.tile([P, 4, P], F32, tag="sh", name="tpx")
                for k in range(4):
                    nc.tensor.transpose(
                        out=tp[:, k, :], in_=xw[:, r * 512 + k * P: r * 512 + (k + 1) * P], identity=ident[:]
                    )
                copy_on(X_EVAC[rl], gv[:, r], tp[:].rearrange("p (g u) b -> p g b u", u=2))

        def fe_quant(i):
            t, half = divmod(i, 2)
            nc.vector.quantize_mx(
                out=fe["xc%d" % t][:, 8 * half:8 * half + 8, :].rearrange("p a b -> p (a b)").bitcast(FP8X4),
                scales=fe["xs%d" % t][:, 8 * half:8 * half + 8, :].rearrange("p a b -> p (a b)"),
                in_=fe["g%d" % t][:, half * 4096:(half + 1) * 4096],
            )

        def fe_mx(i, pair):
            t, half = divmod(i, 2)
            q, j = divmod(t, 2)
            xc = fe["xc%d" % t]
            xs = fe["xs%d" % t]
            u = st[q]["u"]
            jr = 2 * half + pair
            ups = ps_sh.tile([P, 512], F32, tag="sh", name="ups")
            for rr in range(2):
                r = 2 * jr + rr
                for g in range(2):
                    nc.tensor.matmul_mx(
                        out=ups[:, rr * 256:(rr + 1) * 256],
                        lhsT=xc[:, 2 * r + g, :].bitcast(FP8X4),
                        lhsT_scale=xs[:, 2 * r + g, :],
                        rhs=wc[:, r, g * 256:(g + 1) * 256].bitcast(FP8X4),
                        rhs_scale=ws[:, r, g * 256:(g + 1) * 256],
                        start=(g == 0),
                        stop=(g == 1),
                    )
                    nc.tensor.matmul_mx(
                        out=st[q]["sum"][:, j * 256:(j + 1) * 256],
                        lhsT=xc[:, 2 * r + g, :].bitcast(FP8X4),
                        lhsT_scale=xs[:, 2 * r + g, :],
                        rhs=wc[:, r, g * 256:(g + 1) * 256].bitcast(FP8X4),
                        rhs_scale=ws[:, r, g * 256:(g + 1) * 256],
                        start=(r == 0 and g == 0),
                        stop=(r == 7 and g == 1),
                    )
            nc.scalar.copy(out=u[:, j * 2048 + jr * 512: j * 2048 + (jr + 1) * 512], in_=ups[:])
            if j == 1 and jr == 3:
                nc.vector.scalar_tensor_tensor(
                    out=st[q]["s"][:].rearrange("p (j k) -> p j k", j=2),
                    in0=st[q]["sum"][:].rearrange("p (j k) -> p j k", j=2), scalar=1.0 / 16.0,
                    in1=bc[:].unsqueeze(1).to_broadcast([P, 2, 256]), op0=ALU.mult, op1=ALU.add,
                )

        def fe_step(i):
            t, half = divmod(i, 2)
            if i < 16 and half == 0:
                if t + 1 < 8:
                    load_x(t + 1)
                fe["g%d" % t] = big.tile([P, 8192], BF16, tag="big", name="grpx", align_bytes=64)
                fe["xc%d" % t] = xq_pool.tile([P, 16, P], U32, tag="xc", name="xc", align_bytes=64)
                fe["xs%d" % t] = xq_pool.tile([P, 16, P], U8, tag="xs", name="xs", align_bytes=64)
                if t % 2 == 0:
                    st[t // 2]["u"] = u_pool.tile([P, 4096], F32, tag="u", name="u")
                    st[t // 2]["s"] = un.tile([P, 512], F32, tag="s1", name="s1")
                    st[t // 2]["sum"] = ps_lg.tile([P, 512], F32, tag="lg", name="sum1")
            for pair in range(2):
                if i < 16:
                    fe_transposes(i, pair)
                if i > 0:
                    fe_mx(i - 1, pair)
            if i < 16:
                fe_quant(i)

        count = [0]

        def turn(dst, src, first, last):
            count[0] = count[0] + 1
            nc.tensor.matmul(
                out=dst, lhsT=src, rhs=ident[:],
                is_transpose=(REG_EVERY == 0 or count[0] % REG_EVERY != 0),
                start=first, stop=last,
            )

        def acc_transposes(dst, srcs):
            n = len(srcs)
            for i in range(n):
                turn(dst, srcs[i], i == 0, i == n - 1)

        def s_mult(q, j):
            d = st[q]
            if j == 0:
                d["p"] = big.tile([P, 4096], F32, tag="big", name="p_s", align_bytes=64)
            pv = d["p"][:].rearrange("p (a h o c) -> p a h o c", a=16, h=2, c=16)
            uv = d["u"][:].rearrange("p (a h o c) -> p a h o c", a=16, h=2, c=16)
            cv = d["td"][:].rearrange("p (a c) -> p a c", c=16)
            for h in range(2):
                eng = nc.gpsimd if S_MULT[2 * j + h] == "G" else nc.vector
                eng.tensor_tensor(
                    out=pv[:, 8 * j:8 * j + 8, h],
                    in0=uv[:, 8 * j:8 * j + 8, h],
                    in1=cv[:, 8 * j:8 * j + 8, :].unsqueeze(2).to_broadcast([P, 8, 8, 16]),
                    op=ALU.mult,
                )

        def s_acc(q, k, j):
            d = st[q]
            src = d["u"] if k == 0 else d["p"]
            sv = src[:].rearrange("p (j r h k) -> p j r h k", j=2, r=8, h=2)
            if j == 0:
                d["acc"] = ps_sh.tile([P, 2, 2, P], F32, tag="sh", name="acc_s")
            for h in range(2):
                acc_transposes(d["acc"][:, j, h, :], [sv[:, j, r, h, :] for r in range(8)])

        def s_evac(q, k):
            d = st[q]
            d["ta"] = un.tile([P, 512], F32, tag="ta", name="ta")
            tv = d["ta"][:].rearrange("p (j h b) -> p j h b", j=2, h=2)
            for h in range(2):
                nc.scalar.activation(
                    out=tv[:, :, h, :], in_=d["acc"][:, :, h, :], func=ACT.Identity,
                    bias=bias_t[:, h:h + 1], scale=(1.0 / 16.0 if k == 0 else 1.0),
                )

        def s_back(q):
            d = st[q]
            d["s"] = ps_lg.tile([P, 512], F32, tag="lg", name="back_s")
            for jh in range(4):
                turn(d["s"][:, jh * P:(jh + 1) * P], d["ta"][:, jh * P:(jh + 1) * P], True, True)

        def sq_square(q, k):
            d = st[q]
            if k == 0:
                d["ta"] = un.tile([P, 512], F32, tag="ta", name="ta")
            nc.scalar.activation(out=d["ta"][:], in_=d["s"][:], func=ACT.Square)

        def sq_n2(q):
            d = st[q]
            d["n2"] = un.tile([P, 32], F32, tag="n2", name="n2")
            nc.vector.tensor_reduce(
                out=d["n2"][:].rearrange("p (j c) -> p j c", j=2),
                in_=d["ta"][:].rearrange("p (j o c) -> p j c o", j=2, c=16),
                axis=AX.X, op=ALU.add,
            )
            d["rd"] = un.tile([P, 32], F32, tag="rd", name="rd")
            nc.vector.tensor_scalar(out=d["rd"][:], in0=d["n2"][:], scalar1=1.0 + EPS, scalar2=None, op0=ALU.add)
            nc.vector.reciprocal(out=d["rd"][:], in_=d["rd"][:])

        def sq_sqrt(q):
            d = st[q]
            d["nn"] = un.tile([P, 32], F32, tag="nn", name="nn")
            nc.scalar.activation(out=d["nn"][:], in_=d["n2"][:], func=ACT.Sqrt, bias=tinyb[:, 0:1])

        def sq_gain(q):
            d = st[q]
            d["gain"] = un.tile([P, 32], F32, tag="gain", name="gain")
            nc.vector.tensor_mul(out=d["gain"][:], in0=d["nn"][:], in1=d["rd"][:])

        def a_mult(q, j):
            d = st[q]
            if j == 0:
                d["pa"] = big.tile([P, 4096], F32, tag="big", name="p_a", align_bytes=64)
            pv = d["pa"][:].rearrange("p (j o r c) -> p j o r c", j=2, o=16, c=16)
            uv = d["u"][:].rearrange("p (j r o c) -> p j o r c", j=2, r=8, c=16)
            sv = d["s"][:].rearrange("p (j o c) -> p j o c", j=2, c=16)
            for oh in range(2):
                nc.vector.tensor_tensor(
                    out=pv[:, j, 8 * oh:8 * oh + 8],
                    in0=uv[:, j, 8 * oh:8 * oh + 8],
                    in1=sv[:, j, 8 * oh:8 * oh + 8, :].unsqueeze(2).to_broadcast([P, 8, 8, 16]),
                    op=ALU.mult,
                )

        def a_acc(q, k, j):
            d = st[q]
            if k in A_RED_V:
                if j == 0:
                    d["araw"] = un.tile([P, 256], F32, tag="tb", name="araw_sb")
                nc.vector.tensor_reduce(
                    out=d["araw"][:, j * P:(j + 1) * P],
                    in_=d["pa"][:, j * 2048:(j + 1) * 2048].rearrange("p (o k) -> p k o", o=16),
                    axis=AX.X, op=ALU.add,
                )
                return
            pk = d["pa"][:].rearrange("p (j o k) -> p j o k", j=2, o=16)
            if j == 0:
                d["acca"] = ps_sh.tile([P, 2, P], F32, tag="sh", name="acc_a")
            acc_transposes(d["acca"][:, j, :], [pk[:, j, o, :] for o in range(16)])

        def a_evac(q):
            d = st[q]
            d["tb"] = un.tile([P, 256], F32, tag="tb", name="tb")
            nc.scalar.copy(out=d["tb"][:].rearrange("p (j b) -> p j b", j=2), in_=d["acca"][:])

        def a_back(q):
            d = st[q]
            d["araw"] = ps_sh.tile([P, 256], F32, tag="sh", name="back_a")
            for j in range(2):
                turn(d["araw"][:, j * P:(j + 1) * P], d["tb"][:, j * P:(j + 1) * P], True, True)

        def a_logit(q, k):
            d = st[q]
            gv = d["gain"][:].rearrange("p (j c) -> p j c", j=2).unsqueeze(2).to_broadcast([P, 2, 8, 16])
            av = d["araw"][:].rearrange("p (j r c) -> p j r c", j=2, c=16)
            if k == 0:
                d["logit"] = un.tile([P, 256], F32, tag="logit", name="logit")
                nc.vector.tensor_tensor(
                    out=d["logit"][:].rearrange("p (j r c) -> p j r c", j=2, c=16), in0=av, in1=gv, op=ALU.mult
                )
            else:
                tmp = d["araw"] if k in A_RED_V else d["tb"]
                nc.vector.tensor_tensor(
                    out=tmp[:].rearrange("p (j r c) -> p j r c", j=2, c=16), in0=av, in1=gv, op=ALU.mult
                )
                nc.vector.tensor_add(out=d["logit"][:], in0=tmp[:], in1=d["logit"][:])
            lv = d["logit"][:].rearrange("p (a c) -> p a c", c=16)
            d["mx"] = un.tile([P, 16], F32, tag="mx", name="mx")
            nc.vector.tensor_reduce(out=d["mx"][:], in_=lv, axis=AX.X, op=ALU.max)
            d["td"] = un.tile([P, 256], F32, tag="td", name="td")
            nc.vector.tensor_tensor(
                out=d["td"][:].rearrange("p (a c) -> p a c", c=16), in0=lv,
                in1=d["mx"][:].unsqueeze(2).to_broadcast([P, 16, 16]), op=ALU.subtract,
            )

        def a_exp(q):
            d = st[q]
            nc.scalar.activation(out=d["td"][:], in_=d["td"][:], func=ACT.Exp)

        def a_soft(q):
            d = st[q]
            ev = d["td"][:].rearrange("p (a c) -> p a c", c=16)
            nc.vector.tensor_reduce(out=d["mx"][:], in_=ev, axis=AX.X, op=ALU.add)
            nc.vector.reciprocal(out=d["mx"][:], in_=d["mx"][:])
            nc.vector.tensor_tensor(
                out=ev, in0=ev, in1=d["mx"][:].unsqueeze(2).to_broadcast([P, 16, 16]), op=ALU.mult
            )

        def out_v(q):
            d = st[q]
            nc.vector.tensor_tensor(
                out=d["ta"][:].rearrange("p (j c o) -> p j c o", j=2, o=16),
                in0=d["s"][:].rearrange("p (j o c) -> p j c o", j=2, c=16),
                in1=d["gain"][:].rearrange("p (j c) -> p j c", j=2).unsqueeze(3).to_broadcast([P, 2, 16, 16]),
                op=ALU.mult,
            )
            nc.sync.dma_start(
                out=out[q * 256:(q + 1) * 256].rearrange("(j b) c o -> b j (c o)", j=2),
                in_=d["ta"][:].rearrange("p (j k) -> p j k", j=2),
            )

        def routing_steps(q):
            steps = []
            for k in range(3):
                if k > 0:
                    steps.append(lambda: s_mult(q, 0))
                    steps.append(lambda: s_mult(q, 1))
                    steps.append(lambda k=k: s_acc(q, k, 0))
                    steps.append(lambda k=k: s_acc(q, k, 1))
                    steps.append(lambda k=k: s_evac(q, k))
                    steps.append(lambda: s_back(q))
                steps.append(lambda k=k: sq_square(q, k))
                if k < 2:
                    steps.append(lambda: a_mult(q, 0))
                    steps.append(lambda: sq_n2(q))
                    steps.append(lambda: a_mult(q, 1))
                    steps.append(lambda k=k: a_acc(q, k, 0))
                    steps.append(lambda: sq_sqrt(q))
                    steps.append(lambda k=k: a_acc(q, k, 1))
                    steps.append(lambda: sq_gain(q))
                    if k not in A_RED_V:
                        steps.append(lambda: a_evac(q))
                        steps.append(lambda: a_back(q))
                    steps.append(lambda k=k: a_logit(q, k))
                    steps.append(lambda: a_exp(q))
                    steps.append(lambda: a_soft(q))
                else:
                    steps.append(lambda: sq_n2(q))
                    steps.append(lambda: sq_sqrt(q))
                    steps.append(lambda: sq_gain(q))
                    steps.append(lambda: out_v(q))
            return steps

        chains = []

        def advance(n):
            for rep in range(n):
                for ch in chains:
                    if ch[1] < len(ch[0]):
                        ch[0][ch[1]]()
                        ch[1] = ch[1] + 1

        load_w(0)
        load_x(0)
        load_w(1)
        w_step(0)
        w_step(1)
        fe_step(0)
        w_step(2)
        w_step(3)
        for i in range(1, 17):
            fe_step(i)
            if i % 4 == 0:
                chains.append([routing_steps(i // 4 - 1), 0])
            advance(RATE)
        for rep in range(60):
            advance(1)
